import numpy as np
import ml_dtypes


def mxq(x, axis, fmt="e4m3"):
    dtype, down = {"e4m3": (ml_dtypes.float8_e4m3fn, 7), "e5m2": (ml_dtypes.float8_e5m2, 14)}[fmt]
    v = np.moveaxis(np.asarray(x, np.float32).astype(ml_dtypes.bfloat16).astype(np.float64), axis, -1)
    blocks = v.reshape(v.shape[:-1] + (-1, 32))
    amax = np.abs(blocks).max(-1, keepdims=True)
    byte = np.maximum(np.where(amax > 0, np.frexp(amax)[1] - 1 + 127, 0) - down, 1)
    scale = np.exp2(byte - 127.0)
    codes = (blocks / scale).astype(np.float32).astype(dtype).astype(np.float64)
    return np.moveaxis((codes * scale).reshape(v.shape), -1, axis)


WIDE = False


def mx_kscale(k):
    if not WIDE:
        return np.ones(k)
    levels = np.array([10, -10, 5, -5, 0])
    if k % 512:
        return np.exp2(np.random.permutation(np.resize(levels, k // 32))).repeat(32)
    a = np.empty((k // 512, 16))
    for p in range(k // 512):
        a[p, :8] = np.random.permutation(np.resize(levels, 8))
        for g in range(8):
            far = levels[np.abs(levels - a[p, g]) >= 10]
            a[p, g + 8] = far[np.random.randint(len(far))]
    return np.exp2(a.ravel()).repeat(32)


BF16 = ml_dtypes.bfloat16


def bf(x):
    return np.asarray(x, np.float32).astype(BF16)


def f64(x):
    return np.asarray(x).astype(np.float64)


H, D_CONTENT, D_POS, D_K, D_V, B, L = 8, 768, 256, 128, 128, 4, 256
D_MODEL = D_CONTENT + D_POS
T = B * L
DV1 = D_V // 2
KP = H * DV1
EPS = 1e-3


def setup_inputs():
    s1, s2 = mx_kscale(KP), mx_kscale(KP)
    sc = np.concatenate([s1.reshape(H, DV1), s2.reshape(H, DV1)], axis=1)
    return {
        "attn_out": bf(np.random.standard_normal((H, B, L, D_V)) * 0.4 * sc[:, None, None, :]),
        "inp": bf(np.random.standard_normal((T, D_MODEL)) * 0.05 + np.random.standard_normal((T, 1)) * 0.03),
        "w_proj1": bf(np.random.standard_normal((KP, D_CONTENT)) * 0.1 / np.sqrt(KP) / s1[:, None]),
        "w_proj2": bf(np.random.standard_normal((KP, D_POS)) * 0.1 / np.sqrt(KP) / s2[:, None]),
        "ln_a": bf(1.0 + 0.1 * np.random.standard_normal(D_MODEL)),
        "ln_b": bf(0.1 * np.random.standard_normal(D_MODEL)),
    }


def core(attn_out, inp, w_proj1, w_proj2, ln_a, ln_b):
    o = f64(attn_out).reshape(H, T, D_V).transpose(1, 0, 2)
    o1 = o[:, :, :DV1].reshape(T, KP)
    o2 = o[:, :, DV1:].reshape(T, KP)
    y1 = mxq(o1, 1, "e4m3") @ mxq(f64(w_proj1), 0, "e4m3")
    y2 = mxq(o2, 1, "e4m3") @ mxq(f64(w_proj2), 0, "e4m3")
    z = np.concatenate([y1, y2], -1) + f64(inp)
    mu = np.mean(z, axis=-1, keepdims=True)
    sigma = np.std(z, axis=-1, keepdims=True, ddof=1)
    ln = (z - mu) / (sigma + EPS)
    return ln * f64(ln_a) + f64(ln_b)


def e4m3fn_bytes(y):
    return np.clip(np.asarray(y, np.float64), -448.0, 448.0).astype(np.float32).astype(ml_dtypes.float8_e4m3fn).view(np.uint8)


def reference(attn_out, inp, w_proj1, w_proj2, ln_a, ln_b):
    out = core(attn_out, inp, w_proj1, w_proj2, ln_a, ln_b)
    s = np.max(np.abs(out)) / 448.0
    return out, e4m3fn_bytes(out / s)

@@ -1,0 +1,428 @@
+from contextlib import ExitStack
+
+import concourse.mybir as mybir
+from concourse.masks import make_identity
+
+FLOPS = 2 * 1024 * 512 * 1024
+
+F32 = mybir.dt.float32
+BF16 = mybir.dt.bfloat16
+U32 = mybir.dt.uint32
+U8 = mybir.dt.uint8
+FP8X4 = mybir.dt.float8_e4m3fn_x4
+FP8 = mybir.dt.float8_e4m3fn
+ALU = mybir.AluOpType
+ACT = mybir.ActivationFunctionType
+AX = mybir.AxisListType
+
+P = 128
+NT = 8
+D = 1024
+HALF = 512
+H = 8
+EPS = 1e-3
+
+MANUAL = True
+CG = [0, 640, 640, 640, 640, 640, 512, 320]
+CGMAX = 640
+GROUPS = [(0, 1), (1, 2), (2, 4), (4, 6), (6, 8)]
+P2V = [(0, 0, 1024), (1, 0, 1024), (3, 0, 1024), (4, 0, 1024), (6, 0, 1024), (7, 0, 512)]
+P2S = [(2, 0, 1024), (5, 0, 1024), (7, 512, 1024)]
+
+
+def tile_multiheadattention_pa_kernel(tc, attn_out, inp, w_proj1, w_proj2, ln_a, ln_b, out_0, out_1):
+    nc = tc.nc
+    with ExitStack() as ctx:
+        const = ctx.enter_context(tc.tile_pool(name="const", bufs=1))
+        work2 = ctx.enter_context(tc.tile_pool(name="work2", bufs=2))
+        work3 = ctx.enter_context(tc.tile_pool(name="work3", bufs=3))
+        work4 = ctx.enter_context(tc.tile_pool(name="work4", bufs=4))
+        stat = ctx.enter_context(tc.tile_pool(name="stat", bufs=4))
+        psum = ctx.enter_context(tc.psum_pool(name="psum", bufs=2))
+        psum1 = ctx.enter_context(tc.psum_pool(name="psum1", bufs=1))
+        if MANUAL:
+            ctx.enter_context(tc.manual_schedule())
+
+        att = attn_out.rearrange("h b (q i) f -> (b q) h i f", i=NT)
+        inp_v = inp.rearrange("(p i) c -> p i c", i=NT)
+        out0_v = out_0.rearrange("(p i) c -> p i c", i=NT)
+        out1_v = out_1.rearrange("(p i) c -> p i c", i=NT)
+        w1_v = w_proj1.rearrange("(p j) c -> p j c", j=4)
+        w2_v = w_proj2.rearrange("(p j) c -> p j c", j=4)
+
+        ab_row = const.tile([P, 2 * D], BF16, name="ab_row")
+        nc.vector.memset(ab_row[:].bitcast(F32), 0.0)
+        warm = const.tile([P, 1], F32, name="warm")
+        warm2 = const.tile([P, 1], F32, name="warm2")
+        nc.vector.memset(warm[:], 1.0)
+        nc.scalar.activation(out=warm2[:], in_=warm[:], func=ACT.Sqrt)
+        ones = const.tile([P, P], BF16, name="ones")
+        nc.vector.memset(ones[:], 1.0)
+        ident = const.tile([P, P], F32, name="ident")
+        make_identity(nc, ident[:])
+
+        w1a = const.tile([P, 4, 512], BF16, name="w1a")
+        w1b = const.tile([P, 4, 256], BF16, name="w1b")
+        w2r = const.tile([P, 4, 256], BF16, name="w2r")
+        xs = []
+        ins = []
+        for g, (i0, i1) in enumerate(GROUPS):
+            xg = const.tile([P, H, i1 - i0, P], BF16, name="xs%d" % g)
+            ig = const.tile([P, i1 - i0, D], BF16, name="in%d" % g)
+            xs.append(xg)
+            ins.append(ig)
+
+        def load_x(g):
+            i0, i1 = GROUPS[g]
+            nc.sync.dma_start(out=xs[g][:], in_=att[:, :, i0:i1, :])
+
+        def load_i(g):
+            i0, i1 = GROUPS[g]
+            nc.sync.dma_start(out=ins[g][:], in_=inp_v[:, i0:i1, :])
+
+        nc.sync.dma_start(out=w1a[:], in_=w1_v[:, :, 0:512])
+        load_x(0)
+        nc.sync.dma_start(out=ab_row[0:1, 0:D], in_=ln_a.rearrange("(o c) -> o c", o=1))
+        nc.sync.dma_start(out=ab_row[0:1, D : 2 * D], in_=ln_b.rearrange("(o c) -> o c", o=1))
+        nc.sync.dma_start(out=w1b[:], in_=w1_v[:, :, 512:768])
+        nc.sync.dma_start(out=w2r[:], in_=w2_v)
+        load_x(1)
+        load_i(0)
+        load_x(2)
+        load_i(1)
+        load_x(3)
+        load_i(2)
+        load_x(4)
+        load_i(3)
+        load_i(4)
+
+        group_of = {}
+        for g, (i0, i1) in enumerate(GROUPS):
+            for i in range(i0, i1):
+                group_of[i] = (g, i - i0)
+
+        a_sb = const.tile([P, CGMAX], BF16, name="a_sb")
+        b_sb = const.tile([P, CGMAX], BF16, name="b_sb")
+        a_ps = psum1.tile([P, D], BF16, name="a_ps")
+        b_ps = psum1.tile([P, D], BF16, name="b_ps")
+        rowmax = const.tile([P, NT + 1], F32, name="rowmax")
+
+        wgA = const.tile([P, 512, 4], BF16, name="wgA", align_bytes=64)
+        wgB = const.tile([P, 512, 4], BF16, name="wgB", align_bytes=64)
+        wcA = const.tile([P, 512], U32, name="wcA", align_bytes=64)
+        wcB = const.tile([P, 512], U32, name="wcB", align_bytes=64)
+        wsA = const.tile([P, 512], U8, name="wsA", align_bytes=64)
+        wsB = const.tile([P, 512], U8, name="wsB", align_bytes=64)
+
+        o_t = []
+        for i in range(NT):
+            ot = const.tile([P, D], F32, name="o%d" % i)
+            o_t.append(ot)
+
+        xr = {}
+        tp = {}
+        og = {}
+        oc = {}
+        osc = {}
+        yA = {}
+        yB = {}
+        z = {}
+        st = {}
+        t1 = {}
+        nrm = {}
+
+        def ok(i):
+            return 0 <= i < NT
+
+        def reorder(i):
+            if not ok(i):
+                return
+            g, il = group_of[i]
+            xw = xs[g][:].bitcast(F32)
+            t = work2.tile([P, 2, 2, P], F32, name="xr", tag="xr")
+            for s in range(2):
+                nc.scalar.copy(
+                    out=t[:, s, :, :].rearrange("p u (h a) -> p u h a", a=16),
+                    in_=xw[:, :, il, 32 * s : 32 * s + 32].rearrange("p h (a u) -> p u h a", u=2),
+                )
+            xr[i] = t
+
+        def transposes(i):
+            if not ok(i):
+                return
+            t = psum.tile([P, 2, 2, P], F32, name="tp", tag="tp")
+            for s in range(2):
+                for u in range(2):
+                    nc.tensor.transpose(t[:, s, u, :], xr[i][:, s, u, :], ident[:])
+            tp[i] = t
+
+        def copy_out(i):
+            if not ok(i):
+                return
+            t = work2.tile([P, D], BF16, name="og", tag="og", align_bytes=64)
+            nc.scalar.copy(
+                out=t[:].bitcast(F32).rearrange("p (s r u) -> p s r u", s=2, u=2),
+                in_=tp[i][:].rearrange("p s u r -> p s r u"),
+            )
+            og[i] = t
+
+        def quant(i):
+            if not ok(i):
+                return
+            c = work3.tile([P, 256], U32, name="oc", tag="oc", align_bytes=64)
+            s = work3.tile([P, 256], U8, name="osc", tag="osc", align_bytes=64)
+            nc.vector.quantize_mx(out=c[:].bitcast(FP8X4), scales=s[:], in_=og[i][:])
+            oc[i] = c
+            osc[i] = s
+
+        def mm_a(i):
+            ya = psum.tile([P, HALF], F32, name="yA", tag="yA")
+            nc.tensor.matmul_mx(
+                out=ya[:], lhsT=oc[i][:, 0:128].bitcast(FP8X4), lhsT_scale=osc[i][:, 0:128],
+                rhs=wcA[:].bitcast(FP8X4), rhs_scale=wsA[:], start=True, stop=True,
+            )
+            yA[i] = ya
+
+        def mm_b(i):
+            yb = psum.tile([P, HALF], F32, name="yB", tag="yB")
+            nc.tensor.matmul_mx(
+                out=yb[:, 0:256], lhsT=oc[i][:, 0:128].bitcast(FP8X4), lhsT_scale=osc[i][:, 0:128],
+                rhs=wcB[:, 0:256].bitcast(FP8X4), rhs_scale=wsB[:, 0:256], start=True, stop=True,
+            )
+            nc.tensor.matmul_mx(
+                out=yb[:, 256:512], lhsT=oc[i][:, 128:256].bitcast(FP8X4), lhsT_scale=osc[i][:, 128:256],
+                rhs=wcB[:, 256:512].bitcast(FP8X4), rhs_scale=wsB[:, 256:512], start=True, stop=True,
+            )
+            yB[i] = yb
+
+        def mm(i):
+            if not ok(i):
+                return
+            mm_a(i)
+            mm_b(i)
+
+        def resid_a(i):
+            if not ok(i):
+                return
+            g, il = group_of[i]
+            zt = work4.tile([P, D], F32, name="z", tag="z")
+            sums = stat.tile([P, 2], F32, name="sums", tag="sums")
+            nc.vector.scalar_tensor_tensor(
+                out=zt[:, 0:HALF], in0=yA[i][:], scalar=1.0, in1=ins[g][:, il, 0:HALF],
+                op0=ALU.mult, op1=ALU.add, accum_out=sums[:, 0:1],
+            )
+            z[i] = zt
+            st[i] = {"sums": sums}
+
+        def resid_b(i):
+            if not ok(i):
+                return
+            g, il = group_of[i]
+            nc.vector.scalar_tensor_tensor(
+                out=z[i][:, HALF:D], in0=yB[i][:], scalar=1.0, in1=ins[g][:, il, HALF:D],
+                op0=ALU.mult, op1=ALU.add, accum_out=st[i]["sums"][:, 1:2],
+            )
+
+        def neg_mean(i):
+            if not ok(i):
+                return
+            junk2 = stat.tile([P, 2], F32, name="junk2", tag="junk2")
+            negmu = stat.tile([P, 1], F32, name="negmu", tag="negmu")
+            nc.scalar.activation(out=junk2[:], in_=st[i]["sums"][:], func=ACT.Identity, scale=-1.0 / D, accum_out=negmu[:])
+            st[i]["negmu"] = negmu
+
+        def sum_sq(i):
+            if not ok(i):
+                return
+            ssq = stat.tile([P, 1], F32, name="ssq", tag="ssq")
+            sig = stat.tile([P, 1], F32, name="sig", tag="sig")
+            sq = work2.tile([P, D], F32, name="sq", tag="sq")
+            nc.scalar.activation(out=sq[:], in_=z[i][:], func=ACT.Square, bias=st[i]["negmu"][:], scale=1.0, accum_out=ssq[:])
+            nc.scalar.activation(out=sig[:], in_=ssq[:], func=ACT.Sqrt, scale=1.0 / (D - 1))
+            st[i]["sig"] = sig
+
+        def sig_eps(i):
+            if not ok(i):
+                return
+            sige = stat.tile([P, 1], F32, name="sige", tag="sige")
+            nc.vector.tensor_scalar_add(out=sige[:], in0=st[i]["sig"][:], scalar1=EPS)
+            st[i]["sige"] = sige
+
+        def recip(i):
+            if not ok(i):
+                return
+            rstd = stat.tile([P, 1], F32, name="rstd", tag="rstd")
+            nc.vector.reciprocal(out=rstd[:], in_=st[i]["sige"][:])
+            st[i]["rstd"] = rstd
+
+        def v_gain(i):
+            c = CG[i]
+            t = work2.tile([P, D], F32, name="t1", tag="t1")
+            nc.vector.scalar_tensor_tensor(
+                out=t[:, c:D], in0=z[i][:, c:D], scalar=st[i]["negmu"][:], in1=a_ps[:, c:D], op0=ALU.add, op1=ALU.mult
+            )
+            t1[i] = t
+
+        def v_bias(i):
+            c = CG[i]
+            nc.vector.scalar_tensor_tensor(
+                out=o_t[i][:, c:D], in0=t1[i][:, c:D], scalar=st[i]["rstd"][:], in1=b_ps[:, c:D], op0=ALU.mult, op1=ALU.add
+            )
+
+        def s_norm(i):
+            if not ok(i) or CG[i] == 0:
+                return
+            c = CG[i]
+            nmr = stat.tile([P, 1], F32, name="nmr", tag="nmr")
+            t = work2.tile([P, CGMAX], F32, name="nrm", tag="nrm")
+            nc.scalar.activation(out=nmr[:], in_=st[i]["negmu"][:], func=ACT.Copy, scale=st[i]["rstd"][:])
+            nc.scalar.activation(out=t[:, 0:c], in_=z[i][:, 0:c], func=ACT.Identity, scale=st[i]["rstd"][:], bias=nmr[:])
+            nrm[i] = t
+
+        def g_affine(i):
+            if not ok(i) or CG[i] == 0:
+                return
+            c = CG[i]
+            t = work2.tile([P, CGMAX], F32, name="t2", tag="t2")
+            nc.gpsimd.tensor_tensor(out=t[:, 0:c], in0=nrm[i][:, 0:c], in1=a_sb[:, 0:c], op=ALU.mult)
+            nc.gpsimd.tensor_tensor(out=o_t[i][:, 0:c], in0=t[:, 0:c], in1=b_sb[:, 0:c], op=ALU.add)
+
+        def amax_part(i, c0, c1, col):
+            nc.vector.tensor_reduce(
+                out=rowmax[:, col : col + 1], in_=o_t[i][:, c0:c1], axis=AX.X, op=ALU.max, apply_absolute_value=True
+            )
+
+        def amax_row(i):
+            if not ok(i):
+                return
+            amax_part(i, 0, D, i)
+
+        def store0(i):
+            if not ok(i):
+                return
+            nc.sync.dma_start(out=out0_v[:, i, :], in_=o_t[i][:])
+
+        def spread(dst, col0):
+            for k in range(2):
+                nc.tensor.matmul(
+                    out=dst[:, k * HALF : (k + 1) * HALF], lhsT=ones[:],
+                    rhs=ab_row[:, col0 + k * HALF : col0 + (k + 1) * HALF], start=True, stop=True,
+                )
+
+        nc.vector.tensor_copy(out=wgA[:], in_=w1a[:].rearrange("p j c -> p c j"))
+        nc.vector.quantize_mx(out=wcA[:].bitcast(FP8X4), scales=wsA[:], in_=wgA[:].rearrange("p c j -> p (c j)"))
+        reorder(0)
+        transposes(0)
+        copy_out(0)
+        nc.vector.tensor_copy(out=wgB[:, 0:256, :], in_=w1b[:].rearrange("p j c -> p c j"))
+        quant(0)
+        nc.vector.tensor_copy(out=wgB[:, 256:512, :], in_=w2r[:].rearrange("p j c -> p c j"))
+        nc.vector.quantize_mx(out=wcB[:].bitcast(FP8X4), scales=wsB[:], in_=wgB[:].rearrange("p c j -> p (c j)"))
+        spread(a_ps, 0)
+        mm_a(0)
+        reorder(1)
+        transposes(1)
+        mm_b(0)
+        spread(b_ps, D)
+        nc.scalar.copy(out=a_sb[:], in_=a_ps[:, 0:CGMAX])
+        copy_out(1)
+        resid_a(0)
+        resid_b(0)
+        reorder(2)
+        transposes(2)
+        neg_mean(0)
+        quant(1)
+        mm(1)
+        reorder(3)
+        v_gain(0)
+        sum_sq(0)
+        copy_out(2)
+        transposes(3)
+        resid_a(1)
+        sig_eps(0)
+        resid_b(1)
+        recip(0)
+        neg_mean(1)
+        quant(2)
+        mm(2)
+        v_bias(0)
+        nc.scalar.copy(out=b_sb[:], in_=b_ps[:, 0:CGMAX])
+        s_norm(0)
+        g_affine(0)
+        sum_sq(1)
+
+        for s in range(NT):
+            store0(s - 1)
+            copy_out(s + 3)
+            reorder(s + 4)
+            resid_a(s + 2)
+            sig_eps(s + 1)
+            resid_b(s + 2)
+            recip(s + 1)
+            quant(s + 3)
+            mm(s + 3)
+            transposes(s + 4)
+            neg_mean(s + 2)
+            sum_sq(s + 2)
+            s_norm(s + 1)
+            g_affine(s + 1)
+            if s > 0:
+                v_gain(s)
+            amax_row(s - 1)
+            if s > 0:
+                v_bias(s)
+        amax_part(NT - 1, 0, CG[NT - 1], NT - 1)
+        amax_part(NT - 1, CG[NT - 1], D, NT)
+        store0(NT - 1)
+
+        pm = const.tile([P, 1], F32, name="pm")
+        nc.vector.tensor_reduce(out=pm[:], in_=rowmax[:], axis=AX.X, op=ALU.max)
+        pmT = psum.tile([P, P], F32, name="pmT", tag="tp")
+        nc.tensor.transpose(pmT[:], pm[:, 0:1].to_broadcast([P, P]), ident[:])
+        amax = const.tile([P, 1], F32, name="amax")
+        nc.vector.tensor_reduce(out=amax[:], in_=pmT[:], axis=AX.X, op=ALU.max)
+        ramax = const.tile([P, 1], F32, name="ramax")
+        nc.vector.reciprocal(out=ramax[:], in_=amax[:])
+        r = const.tile([P, 1], F32, name="r")
+        nc.vector.tensor_scalar_mul(out=r[:], in0=ramax[:], scalar1=448.0)
+
+        f8 = []
+        for i in range(NT):
+            ft = const.tile([P, D], FP8, name="f8_%d" % i)
+            f8.append(ft)
+
+        scv = {}
+        scs = {}
+
+        def v_scale(k):
+            i, c0, c1 = P2V[k]
+            t = work3.tile([P, D], F32, name="scv", tag="scv")
+            nc.vector.tensor_scalar_mul(out=t[:, 0 : c1 - c0], in0=o_t[i][:, c0:c1], scalar1=r[:])
+            scv[k] = t
+
+        def v_cast(k):
+            i, c0, c1 = P2V[k]
+            nc.vector.tensor_copy(out=f8[i][:, c0:c1], in_=scv[k][:, 0 : c1 - c0], saturate=False)
+
+        def s_scale(k):
+            i, c0, c1 = P2S[k]
+            t = work3.tile([P, D], F32, name="scs", tag="scs")
+            nc.scalar.activation(out=t[:, 0 : c1 - c0], in_=o_t[i][:, c0:c1], func=ACT.Copy, scale=r[:])
+            scs[k] = t
+
+        def s_cast(k):
+            i, c0, c1 = P2S[k]
+            nc.scalar.copy(out=f8[i][:, c0:c1], in_=scs[k][:, 0 : c1 - c0], saturate=False)
+
+        v_scale(0)
+        for k in range(len(P2V)):
+            if k + 1 < len(P2V):
+                v_scale(k + 1)
+            v_cast(k)
+        s_scale(0)
+        for k in range(len(P2S)):
+            if k + 1 < len(P2S):
+                s_scale(k + 1)
+            s_cast(k)
+        for i in range(NT):
+            nc.sync.dma_start(out=out1_v[:, i, :], in_=f8[i][:].bitcast(U8))

@@ -22,7 +22,8 @@ HALF = 512
 H = 8
 EPS = 1e-3
 
-MANUAL = True
+MANUAL = False
+GSPLIT = 2
 CG = [0, 640, 640, 640, 640, 640, 512, 320]
 CGMAX = 640
 GROUPS = [(0, 1), (1, 2), (2, 4), (4, 6), (6, 8)]
@@ -139,21 +140,18 @@ def tile_multiheadattention_pa_kernel(tc, attn_out, inp, w_proj1, w_proj2, ln_a,
                 return
             g, il = group_of[i]
             xw = xs[g][:].bitcast(F32)
-            t = work2.tile([P, 2, 2, P], F32, name="xr", tag="xr")
-            for s in range(2):
-                nc.scalar.copy(
-                    out=t[:, s, :, :].rearrange("p u (h a) -> p u h a", a=16),
-                    in_=xw[:, :, il, 32 * s : 32 * s + 32].rearrange("p h (a u) -> p u h a", u=2),
-                )
+            t = work2.tile([P, 2, H, 32], F32, name="xr", tag="xr")
+            nc.scalar.copy(out=t[:], in_=xw[:, :, il, :].rearrange("p h (s w) -> p s h w", s=2))
             xr[i] = t
 
         def transposes(i):
             if not ok(i):
                 return
             t = psum.tile([P, 2, 2, P], F32, name="tp", tag="tp")
+            words = xr[i][:].rearrange("p s h w -> p (s h w)")
             for s in range(2):
                 for u in range(2):
-                    nc.tensor.transpose(t[:, s, u, :], xr[i][:, s, u, :], ident[:])
+                    nc.tensor.transpose(t[:, s, u, :], words[:, 256 * s + u : 256 * (s + 1) : 2], ident[:])
             tp[i] = t
 
         def copy_out(i):
@@ -238,14 +236,9 @@ def tile_multiheadattention_pa_kernel(tc, attn_out, inp, w_proj1, w_proj2, ln_a,
             sig = stat.tile([P, 1], F32, name="sig", tag="sig")
             sq = work2.tile([P, D], F32, name="sq", tag="sq")
             nc.scalar.activation(out=sq[:], in_=z[i][:], func=ACT.Square, bias=st[i]["negmu"][:], scale=1.0, accum_out=ssq[:])
-            nc.scalar.activation(out=sig[:], in_=ssq[:], func=ACT.Sqrt, scale=1.0 / (D - 1))
-            st[i]["sig"] = sig
-
-        def sig_eps(i):
-            if not ok(i):
-                return
             sige = stat.tile([P, 1], F32, name="sige", tag="sige")
-            nc.vector.tensor_scalar_add(out=sige[:], in0=st[i]["sig"][:], scalar1=EPS)
+            nc.scalar.activation(out=sig[:], in_=ssq[:], func=ACT.Sqrt, scale=1.0 / (D - 1))
+            nc.scalar.activation(out=sige[:], in_=sig[:], func=ACT.Copy, bias=EPS, scale=1.0)
             st[i]["sige"] = sige
 
         def recip(i):
@@ -284,8 +277,13 @@ def tile_multiheadattention_pa_kernel(tc, attn_out, inp, w_proj1, w_proj2, ln_a,
                 return
             c = CG[i]
             t = work2.tile([P, CGMAX], F32, name="t2", tag="t2")
-            nc.gpsimd.tensor_tensor(out=t[:, 0:c], in0=nrm[i][:, 0:c], in1=a_sb[:, 0:c], op=ALU.mult)
-            nc.gpsimd.tensor_tensor(out=o_t[i][:, 0:c], in0=t[:, 0:c], in1=b_sb[:, 0:c], op=ALU.add)
+            w = c // GSPLIT
+            for k in range(GSPLIT):
+                cs = slice(k * w, (k + 1) * w)
+                nc.gpsimd.tensor_tensor(out=t[:, cs], in0=nrm[i][:, cs], in1=a_sb[:, cs], op=ALU.mult)
+            for k in range(GSPLIT):
+                cs = slice(k * w, (k + 1) * w)
+                nc.gpsimd.tensor_tensor(out=o_t[i][:, cs], in0=t[:, cs], in1=b_sb[:, cs], op=ALU.add)
 
         def amax_part(i, c0, c1, col):
             nc.vector.tensor_reduce(
@@ -339,7 +337,6 @@ def tile_multiheadattention_pa_kernel(tc, attn_out, inp, w_proj1, w_proj2, ln_a,
         copy_out(2)
         transposes(3)
         resid_a(1)
-        sig_eps(0)
         resid_b(1)
         recip(0)
         neg_mean(1)
@@ -356,7 +353,6 @@ def tile_multiheadattention_pa_kernel(tc, attn_out, inp, w_proj1, w_proj2, ln_a,
             copy_out(s + 3)
             reorder(s + 4)
             resid_a(s + 2)
-            sig_eps(s + 1)
             resid_b(s + 2)
             recip(s + 1)
             quant(s + 3)

@@ -23,7 +23,7 @@ H = 8
 EPS = 1e-3
 
 MANUAL = False
-GSPLIT = 2
+GSPLIT = 1
 CG = [0, 640, 640, 640, 640, 640, 512, 320]
 CGMAX = 640
 GROUPS = [(0, 1), (1, 2), (2, 4), (4, 6), (6, 8)]

@@ -24,8 +24,8 @@ EPS = 1e-3
 
 MANUAL = False
 GSPLIT = 1
-CG = [0, 640, 640, 640, 640, 640, 512, 320]
-CGMAX = 640
+CG = [0,512,512,512,512,512,448,256]
+CGMAX = 512
 GROUPS = [(0, 1), (1, 2), (2, 4), (4, 6), (6, 8)]
 P2V = [(0, 0, 1024), (1, 0, 1024), (3, 0, 1024), (4, 0, 1024), (6, 0, 1024), (7, 0, 512)]
 P2S = [(2, 0, 1024), (5, 0, 1024), (7, 512, 1024)]
@@ -250,6 +250,8 @@ def tile_multiheadattention_pa_kernel(tc, attn_out, inp, w_proj1, w_proj2, ln_a,
 
         def v_gain(i):
             c = CG[i]
+            if c == D:
+                return
             t = work2.tile([P, D], F32, name="t1", tag="t1")
             nc.vector.scalar_tensor_tensor(
                 out=t[:, c:D], in0=z[i][:, c:D], scalar=st[i]["negmu"][:], in1=a_ps[:, c:D], op0=ALU.add, op1=ALU.mult
@@ -258,6 +260,8 @@ def tile_multiheadattention_pa_kernel(tc, attn_out, inp, w_proj1, w_proj2, ln_a,
 
         def v_bias(i):
             c = CG[i]
+            if c == D:
+                return
             nc.vector.scalar_tensor_tensor(
                 out=o_t[i][:, c:D], in0=t1[i][:, c:D], scalar=st[i]["rstd"][:], in1=b_ps[:, c:D], op0=ALU.mult, op1=ALU.add
             )

@@ -24,8 +24,9 @@ EPS = 1e-3
 
 MANUAL = False
 GSPLIT = 1
-CG = [0,512,512,512,512,512,448,256]
-CGMAX = 512
+WV = 352
+CG = [0,576,576,576,576,576,512,320]
+CGMAX = 576
 GROUPS = [(0, 1), (1, 2), (2, 4), (4, 6), (6, 8)]
 P2V = [(0, 0, 1024), (1, 0, 1024), (3, 0, 1024), (4, 0, 1024), (6, 0, 1024), (7, 0, 512)]
 P2S = [(2, 0, 1024), (5, 0, 1024), (7, 512, 1024)]
@@ -311,14 +312,16 @@ def tile_multiheadattention_pa_kernel(tc, attn_out, inp, w_proj1, w_proj2, ln_a,
                     rhs=ab_row[:, col0 + k * HALF : col0 + (k + 1) * HALF], start=True, stop=True,
                 )
 
-        nc.vector.tensor_copy(out=wgA[:], in_=w1a[:].rearrange("p j c -> p c j"))
+        nc.vector.tensor_copy(out=wgA[:, 0:WV, :], in_=w1a[:, :, 0:WV].rearrange("p j c -> p c j"))
+        nc.scalar.copy(out=wgA[:, WV:512, :], in_=w1a[:, :, WV:512].rearrange("p j c -> p c j"))
         nc.vector.quantize_mx(out=wcA[:].bitcast(FP8X4), scales=wsA[:], in_=wgA[:].rearrange("p c j -> p (c j)"))
         reorder(0)
         transposes(0)
         copy_out(0)
         nc.vector.tensor_copy(out=wgB[:, 0:256, :], in_=w1b[:].rearrange("p j c -> p c j"))
         quant(0)
-        nc.vector.tensor_copy(out=wgB[:, 256:512, :], in_=w2r[:].rearrange("p j c -> p c j"))
+        nc.vector.tensor_copy(out=wgB[:, 256 : WV, :], in_=w2r[:, :, 0 : WV - 256].rearrange("p j c -> p c j"))
+        nc.scalar.copy(out=wgB[:, WV:512, :], in_=w2r[:, :, WV - 256 : 256].rearrange("p j c -> p c j"))
         nc.vector.quantize_mx(out=wcB[:].bitcast(FP8X4), scales=wsB[:], in_=wgB[:].rearrange("p c j -> p (c j)"))
         spread(a_ps, 0)
         mm_a(0)

from contextlib import ExitStack

import concourse.mybir as mybir
from concourse.masks import make_identity

FLOPS = 2 * 1024 * 512 * 1024

F32 = mybir.dt.float32
BF16 = mybir.dt.bfloat16
U32 = mybir.dt.uint32
U8 = mybir.dt.uint8
FP8X4 = mybir.dt.float8_e4m3fn_x4
FP8 = mybir.dt.float8_e4m3fn
ALU = mybir.AluOpType
ACT = mybir.ActivationFunctionType
AX = mybir.AxisListType

P = 128
NT = 8
D = 1024
HALF = 512
H = 8
EPS = 1e-3

MANUAL = False
GSPLIT = 1
WV = 352
CG = [0,576,576,576,576,576,512,320]
CGMAX = 576
GROUPS = [(0, 1), (1, 2), (2, 4), (4, 6), (6, 8)]
P2V = [(0, 0, 1024), (1, 0, 1024), (3, 0, 1024), (4, 0, 1024), (6, 0, 1024), (7, 0, 512)]
P2S = [(2, 0, 1024), (5, 0, 1024), (7, 512, 1024)]


def tile_multiheadattention_pa_kernel(tc, attn_out, inp, w_proj1, w_proj2, ln_a, ln_b, out_0, out_1):
    nc = tc.nc
    with ExitStack() as ctx:
        const = ctx.enter_context(tc.tile_pool(name="const", bufs=1))
        work2 = ctx.enter_context(tc.tile_pool(name="work2", bufs=2))
        work3 = ctx.enter_context(tc.tile_pool(name="work3", bufs=3))
        work4 = ctx.enter_context(tc.tile_pool(name="work4", bufs=4))
        stat = ctx.enter_context(tc.tile_pool(name="stat", bufs=4))
        psum = ctx.enter_context(tc.psum_pool(name="psum", bufs=2))
        psum1 = ctx.enter_context(tc.psum_pool(name="psum1", bufs=1))
        if MANUAL:
            ctx.enter_context(tc.manual_schedule())

        att = attn_out.rearrange("h b (q i) f -> (b q) h i f", i=NT)
        inp_v = inp.rearrange("(p i) c -> p i c", i=NT)
        out0_v = out_0.rearrange("(p i) c -> p i c", i=NT)
        out1_v = out_1.rearrange("(p i) c -> p i c", i=NT)
        w1_v = w_proj1.rearrange("(p j) c -> p j c", j=4)
        w2_v = w_proj2.rearrange("(p j) c -> p j c", j=4)

        ab_row = const.tile([P, 2 * D], BF16, name="ab_row")
        nc.vector.memset(ab_row[:].bitcast(F32), 0.0)
        warm = const.tile([P, 1], F32, name="warm")
        warm2 = const.tile([P, 1], F32, name="warm2")
        nc.vector.memset(warm[:], 1.0)
        nc.scalar.activation(out=warm2[:], in_=warm[:], func=ACT.Sqrt)
        ones = const.tile([P, P], BF16, name="ones")
        nc.vector.memset(ones[:], 1.0)
        ident = const.tile([P, P], F32, name="ident")
        make_identity(nc, ident[:])

        w1a = const.tile([P, 4, 512], BF16, name="w1a")
        w1b = const.tile([P, 4, 256], BF16, name="w1b")
        w2r = const.tile([P, 4, 256], BF16, name="w2r")
        xs = []
        ins = []
        for g, (i0, i1) in enumerate(GROUPS):
            xg = const.tile([P, H, i1 - i0, P], BF16, name="xs%d" % g)
            ig = const.tile([P, i1 - i0, D], BF16, name="in%d" % g)
            xs.append(xg)
            ins.append(ig)

        def load_x(g):
            i0, i1 = GROUPS[g]
            nc.sync.dma_start(out=xs[g][:], in_=att[:, :, i0:i1, :])

        def load_i(g):
            i0, i1 = GROUPS[g]
            nc.sync.dma_start(out=ins[g][:], in_=inp_v[:, i0:i1, :])

        nc.sync.dma_start(out=w1a[:], in_=w1_v[:, :, 0:512])
        load_x(0)
        nc.sync.dma_start(out=ab_row[0:1, 0:D], in_=ln_a.rearrange("(o c) -> o c", o=1))
        nc.sync.dma_start(out=ab_row[0:1, D : 2 * D], in_=ln_b.rearrange("(o c) -> o c", o=1))
        nc.sync.dma_start(out=w1b[:], in_=w1_v[:, :, 512:768])
        nc.sync.dma_start(out=w2r[:], in_=w2_v)
        load_x(1)
        load_i(0)
        load_x(2)
        load_i(1)
        load_x(3)
        load_i(2)
        load_x(4)
        load_i(3)
        load_i(4)

        group_of = {}
        for g, (i0, i1) in enumerate(GROUPS):
            for i in range(i0, i1):
                group_of[i] = (g, i - i0)

        a_sb = const.tile([P, CGMAX], BF16, name="a_sb")
        b_sb = const.tile([P, CGMAX], BF16, name="b_sb")
        a_ps = psum1.tile([P, D], BF16, name="a_ps")
        b_ps = psum1.tile([P, D], BF16, name="b_ps")
        rowmax = const.tile([P, NT + 1], F32, name="rowmax")

        wgA = const.tile([P, 512, 4], BF16, name="wgA", align_bytes=64)
        wgB = const.tile([P, 512, 4], BF16, name="wgB", align_bytes=64)
        wcA = const.tile([P, 512], U32, name="wcA", align_bytes=64)
        wcB = const.tile([P, 512], U32, name="wcB", align_bytes=64)
        wsA = const.tile([P, 512], U8, name="wsA", align_bytes=64)
        wsB = const.tile([P, 512], U8, name="wsB", align_bytes=64)

        o_t = []
        for i in range(NT):
            ot = const.tile([P, D], F32, name="o%d" % i)
            o_t.append(ot)

        xr = {}
        tp = {}
        og = {}
        oc = {}
        osc = {}
        yA = {}
        yB = {}
        z = {}
        st = {}
        t1 = {}
        nrm = {}

        def ok(i):
            return 0 <= i < NT

        def reorder(i):
            if not ok(i):
                return
            g, il = group_of[i]
            xw = xs[g][:].bitcast(F32)
            t = work2.tile([P, 2, H, 32], F32, name="xr", tag="xr")
            nc.scalar.copy(out=t[:], in_=xw[:, :, il, :].rearrange("p h (s w) -> p s h w", s=2))
            xr[i] = t

        def transposes(i):
            if not ok(i):
                return
            t = psum.tile([P, 2, 2, P], F32, name="tp", tag="tp")
            words = xr[i][:].rearrange("p s h w -> p (s h w)")
            for s in range(2):
                for u in range(2):
                    nc.tensor.transpose(t[:, s, u, :], words[:, 256 * s + u : 256 * (s + 1) : 2], ident[:])
            tp[i] = t

        def copy_out(i):
            if not ok(i):
                return
            t = work2.tile([P, D], BF16, name="og", tag="og", align_bytes=64)
            nc.scalar.copy(
                out=t[:].bitcast(F32).rearrange("p (s r u) -> p s r u", s=2, u=2),
                in_=tp[i][:].rearrange("p s u r -> p s r u"),
            )
            og[i] = t

        def quant(i):
            if not ok(i):
                return
            c = work3.tile([P, 256], U32, name="oc", tag="oc", align_bytes=64)
            s = work3.tile([P, 256], U8, name="osc", tag="osc", align_bytes=64)
            nc.vector.quantize_mx(out=c[:].bitcast(FP8X4), scales=s[:], in_=og[i][:])
            oc[i] = c
            osc[i] = s

        def mm_a(i):
            ya = psum.tile([P, HALF], F32, name="yA", tag="yA")
            nc.tensor.matmul_mx(
                out=ya[:], lhsT=oc[i][:, 0:128].bitcast(FP8X4), lhsT_scale=osc[i][:, 0:128],
                rhs=wcA[:].bitcast(FP8X4), rhs_scale=wsA[:], start=True, stop=True,
            )
            yA[i] = ya

        def mm_b(i):
            yb = psum.tile([P, HALF], F32, name="yB", tag="yB")
            nc.tensor.matmul_mx(
                out=yb[:, 0:256], lhsT=oc[i][:, 0:128].bitcast(FP8X4), lhsT_scale=osc[i][:, 0:128],
                rhs=wcB[:, 0:256].bitcast(FP8X4), rhs_scale=wsB[:, 0:256], start=True, stop=True,
            )
            nc.tensor.matmul_mx(
                out=yb[:, 256:512], lhsT=oc[i][:, 128:256].bitcast(FP8X4), lhsT_scale=osc[i][:, 128:256],
                rhs=wcB[:, 256:512].bitcast(FP8X4), rhs_scale=wsB[:, 256:512], start=True, stop=True,
            )
            yB[i] = yb

        def mm(i):
            if not ok(i):
                return
            mm_a(i)
            mm_b(i)

        def resid_a(i):
            if not ok(i):
                return
            g, il = group_of[i]
            zt = work4.tile([P, D], F32, name="z", tag="z")
            sums = stat.tile([P, 2], F32, name="sums", tag="sums")
            nc.vector.scalar_tensor_tensor(
                out=zt[:, 0:HALF], in0=yA[i][:], scalar=1.0, in1=ins[g][:, il, 0:HALF],
                op0=ALU.mult, op1=ALU.add, accum_out=sums[:, 0:1],
            )
            z[i] = zt
            st[i] = {"sums": sums}

        def resid_b(i):
            if not ok(i):
                return
            g, il = group_of[i]
            nc.vector.scalar_tensor_tensor(
                out=z[i][:, HALF:D], in0=yB[i][:], scalar=1.0, in1=ins[g][:, il, HALF:D],
                op0=ALU.mult, op1=ALU.add, accum_out=st[i]["sums"][:, 1:2],
            )

        def neg_mean(i):
            if not ok(i):
                return
            junk2 = stat.tile([P, 2], F32, name="junk2", tag="junk2")
            negmu = stat.tile([P, 1], F32, name="negmu", tag="negmu")
            nc.scalar.activation(out=junk2[:], in_=st[i]["sums"][:], func=ACT.Identity, scale=-1.0 / D, accum_out=negmu[:])
            st[i]["negmu"] = negmu

        def sum_sq(i):
            if not ok(i):
                return
            ssq = stat.tile([P, 1], F32, name="ssq", tag="ssq")
            sig = stat.tile([P, 1], F32, name="sig", tag="sig")
            sq = work2.tile([P, D], F32, name="sq", tag="sq")
            nc.scalar.activation(out=sq[:], in_=z[i][:], func=ACT.Square, bias=st[i]["negmu"][:], scale=1.0, accum_out=ssq[:])
            sige = stat.tile([P, 1], F32, name="sige", tag="sige")
            nc.scalar.activation(out=sig[:], in_=ssq[:], func=ACT.Sqrt, scale=1.0 / (D - 1))
            nc.scalar.activation(out=sige[:], in_=sig[:], func=ACT.Copy, bias=EPS, scale=1.0)
            st[i]["sige"] = sige

        def recip(i):
            if not ok(i):
                return
            rstd = stat.tile([P, 1], F32, name="rstd", tag="rstd")
            nc.vector.reciprocal(out=rstd[:], in_=st[i]["sige"][:])
            st[i]["rstd"] = rstd

        def v_gain(i):
            c = CG[i]
            if c == D:
                return
            t = work2.tile([P, D], F32, name="t1", tag="t1")
            nc.vector.scalar_tensor_tensor(
                out=t[:, c:D], in0=z[i][:, c:D], scalar=st[i]["negmu"][:], in1=a_ps[:, c:D], op0=ALU.add, op1=ALU.mult
            )
            t1[i] = t

        def v_bias(i):
            c = CG[i]
            if c == D:
                return
            nc.vector.scalar_tensor_tensor(
                out=o_t[i][:, c:D], in0=t1[i][:, c:D], scalar=st[i]["rstd"][:], in1=b_ps[:, c:D], op0=ALU.mult, op1=ALU.add
            )

        def s_norm(i):
            if not ok(i) or CG[i] == 0:
                return
            c = CG[i]
            nmr = stat.tile([P, 1], F32, name="nmr", tag="nmr")
            t = work2.tile([P, CGMAX], F32, name="nrm", tag="nrm")
            nc.scalar.activation(out=nmr[:], in_=st[i]["negmu"][:], func=ACT.Copy, scale=st[i]["rstd"][:])
            nc.scalar.activation(out=t[:, 0:c], in_=z[i][:, 0:c], func=ACT.Identity, scale=st[i]["rstd"][:], bias=nmr[:])
            nrm[i] = t

        def g_affine(i):
            if not ok(i) or CG[i] == 0:
                return
            c = CG[i]
            t = work2.tile([P, CGMAX], F32, name="t2", tag="t2")
            w = c // GSPLIT
            for k in range(GSPLIT):
                cs = slice(k * w, (k + 1) * w)
                nc.gpsimd.tensor_tensor(out=t[:, cs], in0=nrm[i][:, cs], in1=a_sb[:, cs], op=ALU.mult)
            for k in range(GSPLIT):
                cs = slice(k * w, (k + 1) * w)
                nc.gpsimd.tensor_tensor(out=o_t[i][:, cs], in0=t[:, cs], in1=b_sb[:, cs], op=ALU.add)

        def amax_part(i, c0, c1, col):
            nc.vector.tensor_reduce(
                out=rowmax[:, col : col + 1], in_=o_t[i][:, c0:c1], axis=AX.X, op=ALU.max, apply_absolute_value=True
            )

        def amax_row(i):
            if not ok(i):
                return
            amax_part(i, 0, D, i)

        def store0(i):
            if not ok(i):
                return
            nc.sync.dma_start(out=out0_v[:, i, :], in_=o_t[i][:])

        def spread(dst, col0):
            for k in range(2):
                nc.tensor.matmul(
                    out=dst[:, k * HALF : (k + 1) * HALF], lhsT=ones[:],
                    rhs=ab_row[:, col0 + k * HALF : col0 + (k + 1) * HALF], start=True, stop=True,
                )

        nc.vector.tensor_copy(out=wgA[:, 0:WV, :], in_=w1a[:, :, 0:WV].rearrange("p j c -> p c j"))
        nc.scalar.copy(out=wgA[:, WV:512, :], in_=w1a[:, :, WV:512].rearrange("p j c -> p c j"))
        nc.vector.quantize_mx(out=wcA[:].bitcast(FP8X4), scales=wsA[:], in_=wgA[:].rearrange("p c j -> p (c j)"))
        reorder(0)
        transposes(0)
        copy_out(0)
        nc.vector.tensor_copy(out=wgB[:, 0:256, :], in_=w1b[:].rearrange("p j c -> p c j"))
        quant(0)
        nc.vector.tensor_copy(out=wgB[:, 256 : WV, :], in_=w2r[:, :, 0 : WV - 256].rearrange("p j c -> p c j"))
        nc.scalar.copy(out=wgB[:, WV:512, :], in_=w2r[:, :, WV - 256 : 256].rearrange("p j c -> p c j"))
        nc.vector.quantize_mx(out=wcB[:].bitcast(FP8X4), scales=wsB[:], in_=wgB[:].rearrange("p c j -> p (c j)"))
        spread(a_ps, 0)
        mm_a(0)
        reorder(1)
        transposes(1)
        mm_b(0)
        spread(b_ps, D)
        nc.scalar.copy(out=a_sb[:], in_=a_ps[:, 0:CGMAX])
        copy_out(1)
        resid_a(0)
        resid_b(0)
        reorder(2)
        transposes(2)
        neg_mean(0)
        quant(1)
        mm(1)
        reorder(3)
        v_gain(0)
        sum_sq(0)
        copy_out(2)
        transposes(3)
        resid_a(1)
        resid_b(1)
        recip(0)
        neg_mean(1)
        quant(2)
        mm(2)
        v_bias(0)
        nc.scalar.copy(out=b_sb[:], in_=b_ps[:, 0:CGMAX])
        s_norm(0)
        g_affine(0)
        sum_sq(1)

        for s in range(NT):
            store0(s - 1)
            copy_out(s + 3)
            reorder(s + 4)
            resid_a(s + 2)
            resid_b(s + 2)
            recip(s + 1)
            quant(s + 3)
            mm(s + 3)
            transposes(s + 4)
            neg_mean(s + 2)
            sum_sq(s + 2)
            s_norm(s + 1)
            g_affine(s + 1)
            if s > 0:
                v_gain(s)
            amax_row(s - 1)
            if s > 0:
                v_bias(s)
        amax_part(NT - 1, 0, CG[NT - 1], NT - 1)
        amax_part(NT - 1, CG[NT - 1], D, NT)
        store0(NT - 1)

        pm = const.tile([P, 1], F32, name="pm")
        nc.vector.tensor_reduce(out=pm[:], in_=rowmax[:], axis=AX.X, op=ALU.max)
        pmT = psum.tile([P, P], F32, name="pmT", tag="tp")
        nc.tensor.transpose(pmT[:], pm[:, 0:1].to_broadcast([P, P]), ident[:])
        amax = const.tile([P, 1], F32, name="amax")
        nc.vector.tensor_reduce(out=amax[:], in_=pmT[:], axis=AX.X, op=ALU.max)
        ramax = const.tile([P, 1], F32, name="ramax")
        nc.vector.reciprocal(out=ramax[:], in_=amax[:])
        r = const.tile([P, 1], F32, name="r")
        nc.vector.tensor_scalar_mul(out=r[:], in0=ramax[:], scalar1=448.0)

        f8 = []
        for i in range(NT):
            ft = const.tile([P, D], FP8, name="f8_%d" % i)
            f8.append(ft)

        scv = {}
        scs = {}

        def v_scale(k):
            i, c0, c1 = P2V[k]
            t = work3.tile([P, D], F32, name="scv", tag="scv")
            nc.vector.tensor_scalar_mul(out=t[:, 0 : c1 - c0], in0=o_t[i][:, c0:c1], scalar1=r[:])
            scv[k] = t

        def v_cast(k):
            i, c0, c1 = P2V[k]
            nc.vector.tensor_copy(out=f8[i][:, c0:c1], in_=scv[k][:, 0 : c1 - c0], saturate=False)

        def s_scale(k):
            i, c0, c1 = P2S[k]
            t = work3.tile([P, D], F32, name="scs", tag="scs")
            nc.scalar.activation(out=t[:, 0 : c1 - c0], in_=o_t[i][:, c0:c1], func=ACT.Copy, scale=r[:])
            scs[k] = t

        def s_cast(k):
            i, c0, c1 = P2S[k]
            nc.scalar.copy(out=f8[i][:, c0:c1], in_=scs[k][:, 0 : c1 - c0], saturate=False)

        v_scale(0)
        for k in range(len(P2V)):
            if k + 1 < len(P2V):
                v_scale(k + 1)
            v_cast(k)
        s_scale(0)
        for k in range(len(P2S)):
            if k + 1 < len(P2S):
                s_scale(k + 1)
            s_cast(k)
        for i in range(NT):
            nc.sync.dma_start(out=out1_v[:, i, :], in_=f8[i][:].bitcast(U8))
